import numpy as np
import ml_dtypes


def mxq(x, axis, fmt="e4m3"):
    dtype, down = {"e4m3": (ml_dtypes.float8_e4m3fn, 7), "e5m2": (ml_dtypes.float8_e5m2, 14)}[fmt]
    v = np.moveaxis(np.asarray(x, np.float32).astype(ml_dtypes.bfloat16).astype(np.float64), axis, -1)
    blocks = v.reshape(v.shape[:-1] + (-1, 32))
    amax = np.abs(blocks).max(-1, keepdims=True)
    byte = np.maximum(np.where(amax > 0, np.frexp(amax)[1] - 1 + 127, 0) - down, 1)
    scale = np.exp2(byte - 127.0)
    codes = (blocks / scale).astype(np.float32).astype(dtype).astype(np.float64)
    return np.moveaxis((codes * scale).reshape(v.shape), -1, axis)


WIDE = False


def mx_kscale(k):
    if not WIDE:
        return np.ones(k)
    levels = np.array([10, -10, 5, -5, 0])
    if k % 512:
        return np.exp2(np.random.permutation(np.resize(levels, k // 32))).repeat(32)
    a = np.empty((k // 512, 16))
    for p in range(k // 512):
        a[p, :8] = np.random.permutation(np.resize(levels, 8))
        for g in range(8):
            far = levels[np.abs(levels - a[p, g]) >= 10]
            a[p, g + 8] = far[np.random.randint(len(far))]
    return np.exp2(a.ravel()).repeat(32)


BF16 = ml_dtypes.bfloat16


def bf(x):
    return np.asarray(x, np.float32).astype(BF16)


def f64(x):
    return np.asarray(x).astype(np.float64)


B, S, D, HQ, HK, HD = 2, 256, 2048, 16, 8, 128
QD = HQ * HD
KD = HK * HD
E = QD + 2 * KD
EPS = 1e-6
ROPE_BASE = 10000.0
QK_RMS = 0.003


def rope_tables():
    inv_freq = 1.0 / ROPE_BASE ** (np.arange(0, HD, 2) / HD)
    freqs = np.outer(np.arange(S), inv_freq)
    emb = np.concatenate([freqs, freqs], axis=-1)
    return np.cos(emb), np.sin(emb)


def rms_norm(h, w):
    var = np.mean(np.square(h), axis=-1, keepdims=True)
    return h * (1.0 / np.sqrt(var + EPS)) * w


def rotate_half(h):
    h1, h2 = np.split(h, 2, axis=-1)
    return np.concatenate([-h2, h1], axis=-1)


def apply_rope(h, cos, sin):
    return h * cos[None, :, None, :] + rotate_half(h) * sin[None, :, None, :]


def setup_inputs():
    s = mx_kscale(D)
    cos, sin = rope_tables()
    row = np.concatenate([np.full(QD + KD, QK_RMS), np.ones(KD)])
    return {"x": bf(np.random.standard_normal((B, S, D)) * s),
            "pos_cos": bf(cos),
            "pos_sin": bf(sin),
            "w_qkv": bf(np.random.standard_normal((E, D)) * row[:, None] / np.sqrt(D) / s[None, :]),
            "q_norm_w": bf(1.0 + 0.1 * np.random.standard_normal(HD)),
            "k_norm_w": bf(1.0 + 0.1 * np.random.standard_normal(HD))}


def reference(x, pos_cos, pos_sin, w_qkv, q_norm_w, k_norm_w):
    xq = mxq(f64(x), 2, "e4m3")
    wt = f64(w_qkv).T
    q = (xq @ mxq(wt[:, :QD], 0, "e4m3")).reshape(B, S, HQ, HD)
    k = (xq @ mxq(wt[:, QD:QD + KD], 0, "e4m3")).reshape(B, S, HK, HD)
    v = (xq @ mxq(wt[:, QD + KD:], 0, "e4m3")).reshape(B, S, HK, HD)
    cos, sin = f64(pos_cos), f64(pos_sin)
    q = apply_rope(rms_norm(q, f64(q_norm_w)), cos, sin)
    k = apply_rope(rms_norm(k, f64(k_norm_w)), cos, sin)
    return q, k, v

@@ -1,0 +1,260 @@
+from contextlib import ExitStack
+
+import concourse.mybir as mybir
+from concourse.masks import make_identity
+
+F32 = mybir.dt.float32
+BF16 = mybir.dt.bfloat16
+U32 = mybir.dt.uint32
+U8 = mybir.dt.uint8
+FP8X4 = mybir.dt.float8_e4m3fn_x4
+ACT = mybir.ActivationFunctionType
+ALU = mybir.AluOpType
+
+P = 128
+D_MODEL = 2048
+PASSES = 4
+HEAD = 128
+HALF = HEAD // 2
+ROWS = 512
+ROW_TILES = ROWS // P
+HEADS = ROWS // HEAD
+N_GROUPS = 8
+EPS = 1e-6
+
+LOADS_AHEAD = 4
+SHARED_SOURCES = 2
+LAG = 4
+
+FLOPS = 2 * 512 * 4096 * 2048
+
+
+def tile_qwen3attention_pa_kernel(
+    tc, x, pos_cos, pos_sin, w_qkv, q_norm_w, k_norm_w, out_0, out_1, out_2
+):
+    nc = tc.nc
+    with ExitStack() as ctx:
+        ctx.enter_context(tc.manual_schedule())
+        const = ctx.enter_context(tc.tile_pool(name="const", bufs=1))
+        raw_pool = ctx.enter_context(tc.tile_pool(name="raw", bufs=LOADS_AHEAD))
+        grouped_pool = ctx.enter_context(tc.tile_pool(name="grouped", bufs=4))
+        codes_pool = ctx.enter_context(tc.tile_pool(name="codes", bufs=3))
+        small = ctx.enter_context(tc.tile_pool(name="small", bufs=4))
+        scratch = ctx.enter_context(tc.tile_pool(name="scratch", bufs=2))
+        products_pool = ctx.enter_context(tc.tile_pool(name="products", bufs=5))
+        result_pool = ctx.enter_context(tc.tile_pool(name="result", bufs=5))
+        psum_t = ctx.enter_context(tc.psum_pool(name="psum_t", bufs=4))
+        psum_acc = ctx.enter_context(tc.psum_pool(name="psum_acc", bufs=4))
+
+        sources = [x.rearrange("b s d -> (b s) d")]
+        for g in range(N_GROUPS):
+            sources.append(w_qkv[g * ROWS : (g + 1) * ROWS, :])
+        raws = {}
+        codes = {}
+        scales = {}
+
+        def load(s):
+            raw = raw_pool.tile([P, ROW_TILES, D_MODEL], BF16)
+            rows = sources[s].rearrange("(r p) k -> p r k", p=P)
+            for half in range(2):
+                features = slice(half * D_MODEL // 2, (half + 1) * D_MODEL // 2)
+                nc.sync.dma_start(out=raw[:, :, features], in_=rows[:, :, features])
+            raws[s] = raw
+
+        gain_rows = const.tile([P, 2, HEAD], BF16)
+        nc.vector.memset(gain_rows[:], 0.0)
+        nc.sync.dma_start(out=gain_rows[0:1, 0, :], in_=q_norm_w.rearrange("(o d) -> o d", o=1))
+        nc.sync.dma_start(out=gain_rows[0:1, 1, :], in_=k_norm_w.rearrange("(o d) -> o d", o=1))
+        load(0)
+        cos = const.tile([P, 2, HEAD], BF16)
+        sin = const.tile([P, 2, HEAD], BF16)
+        nc.sync.dma_start(out=cos[:], in_=pos_cos.rearrange("(t p) d -> p t d", p=P))
+        nc.sync.dma_start(out=sin[:], in_=pos_sin.rearrange("(t p) d -> p t d", p=P))
+        for s in range(1, LOADS_AHEAD):
+            load(s)
+
+        ident = const.tile([P, P], F32)
+        make_identity(nc, ident[:])
+        eps = const.tile([P, 1], F32)
+        nc.vector.memset(eps[:], EPS)
+        warm = const.tile([P, 1], F32)
+        nc.scalar.activation(out=warm[:], in_=eps[:], func=ACT.Sqrt)
+
+        ones = const.tile([P, P], BF16)
+        nc.vector.memset(ones[:], 1.0)
+        acc = psum_acc.tile([P, ROWS], F32)
+        nc.tensor.matmul(
+            out=acc[:, 0 : 2 * HEAD],
+            lhsT=ones[:],
+            rhs=gain_rows[:].rearrange("p g d -> p (g d)"),
+            start=True,
+            stop=True,
+        )
+        gains = const.tile([P, 2, HEAD], F32)
+        nc.vector.tensor_copy(out=gains[:].rearrange("p g d -> p (g d)"), in_=acc[:, 0 : 2 * HEAD])
+
+        tables = []
+        for kind in range(2):
+            table = const.tile([P, 2, 2, HEAD], F32, name="table%d" % kind)
+            nc.gpsimd.tensor_tensor(
+                out=table[:, :, 0, :],
+                in0=cos[:],
+                in1=gains[:, kind, :].unsqueeze(1).to_broadcast([P, 2, HEAD]),
+                op=ALU.mult,
+            )
+            nc.gpsimd.tensor_tensor(
+                out=table[:, :, 1, 0:HALF],
+                in0=sin[:, :, HALF:HEAD],
+                in1=gains[:, kind, 0:HALF].unsqueeze(1).to_broadcast([P, 2, HALF]),
+                op=ALU.mult,
+            )
+            nc.gpsimd.tensor_tensor(
+                out=table[:, :, 1, HALF:HEAD],
+                in0=sin[:, :, 0:HALF],
+                in1=gains[:, kind, HALF:HEAD].unsqueeze(1).to_broadcast([P, 2, HALF]),
+                op=ALU.mult,
+            )
+            tables.append(table)
+
+        groups = []
+        for out, table in ((out_0, tables[0]), (out_1, tables[1]), (out_2, None)):
+            flat = out.rearrange("b s h d -> (b s) (h d)")
+            for col in range(0, flat.shape[1], ROWS):
+                groups.append((flat[:, col : col + ROWS], table))
+
+        def transpose_half(s, half):
+            if half == 0:
+                pool = const if s == 0 else codes_pool
+                code_words = pool.tile([P, PASSES, ROWS], U32, align_bytes=64)
+                scale_bytes = pool.tile([P, PASSES, ROWS], U8, align_bytes=64)
+                codes[s] = code_words
+                scales[s] = scale_bytes
+            raw_words = raws[s][:].bitcast(F32)
+            made = []
+            for c in (2 * half, 2 * half + 1):
+                grouped = grouped_pool.tile([P, 4 * ROWS], BF16, align_bytes=64)
+                grouped_words = grouped[:].bitcast(F32).rearrange("p (n u) -> p n u", u=2)
+                for pair in range(ROW_TILES // 2):
+                    bank = psum_t.tile([P, 2, 2 * P], F32)
+                    for u in range(2):
+                        for rr in range(2):
+                            first = 2 * c * P + u
+                            nc.tensor.transpose(
+                                bank[:, u, rr * P : (rr + 1) * P],
+                                raw_words[:, 2 * pair + rr, first : first + 2 * P - 1 : 2],
+                                ident[:],
+                            )
+                    copy_out = nc.scalar.copy
+                    if s < SHARED_SOURCES and pair == 1:
+                        copy_out = nc.vector.tensor_copy
+                    copy_out(
+                        out=grouped_words[:, pair * 2 * P : (pair + 1) * 2 * P, :],
+                        in_=bank[:].rearrange("p u n -> p n u"),
+                    )
+                made.append((c, grouped))
+            return made
+
+        def quantise_half(s, made):
+            for c, grouped in made:
+                nc.vector.quantize_mx(
+                    out=codes[s][:, c, :].bitcast(FP8X4),
+                    scales=scales[s][:, c, :],
+                    in_=grouped[:],
+                )
+
+        def matmul_half(g, half):
+            sums = []
+            for m in (2 * half, 2 * half + 1):
+                acc = psum_acc.tile([P, ROWS], F32)
+                sums.append((m, acc))
+            for c in range(PASSES):
+                for m, acc in sums:
+                    nc.tensor.matmul_mx(
+                        out=acc[:],
+                        lhsT=codes[0][:, c, m * P : (m + 1) * P].bitcast(FP8X4),
+                        lhsT_scale=scales[0][:, c, m * P : (m + 1) * P],
+                        rhs=codes[g + 1][:, c, :].bitcast(FP8X4),
+                        rhs_scale=scales[g + 1][:, c, :],
+                        start=(c == 0),
+                        stop=(c == PASSES - 1),
+                    )
+            return sums
+
+        def store(queue, dst, sums, result):
+            first = sums[0][0] * P
+            queue.dma_start(
+                out=dst[first : first + 2 * P, :].rearrange("(b p) f -> p b f", p=P),
+                in_=result[:].rearrange("p (b h) d -> p b (h d)", b=2),
+            )
+
+        def norm_and_rope(g, sums):
+            dst, table = groups[g]
+            sumsq = small.tile([P, 2 * HEADS], F32)
+            squares = scratch.tile([P, 2 * HEADS, HEAD], BF16)
+            for b, (m, acc) in enumerate(sums):
+                for h in range(HEADS):
+                    nc.scalar.activation(
+                        out=squares[:, b * HEADS + h, :],
+                        in_=acc[:, h * HEAD : (h + 1) * HEAD],
+                        func=ACT.Square,
+                        accum_out=sumsq[:, b * HEADS + h : b * HEADS + h + 1],
+                    )
+            rms = small.tile([P, 2 * HEADS], F32)
+            nc.scalar.activation(
+                out=rms[:], in_=sumsq[:], func=ACT.Sqrt, scale=1.0 / HEAD, bias=eps[:, 0:1]
+            )
+            inv_rms = small.tile([P, 2 * HEADS], F32)
+            nc.vector.reciprocal(out=inv_rms[:], in_=rms[:])
+            products = products_pool.tile([P, 2 * HEADS, 2, HEAD], F32)
+            for b, (m, acc) in enumerate(sums):
+                for h in range(HEADS):
+                    nc.vector.scalar_tensor_tensor(
+                        out=products[:, b * HEADS + h, :, :],
+                        in0=acc[:, h * HEAD : (h + 1) * HEAD].unsqueeze(1).to_broadcast([P, 2, HEAD]),
+                        scalar=inv_rms[:, b * HEADS + h : b * HEADS + h + 1],
+                        in1=table[:, m % 2, :, :],
+                        op0=ALU.mult,
+                        op1=ALU.mult,
+                    )
+            result = result_pool.tile([P, 2 * HEADS, HEAD], F32)
+            nc.gpsimd.tensor_tensor(
+                out=result[:, :, 0:HALF],
+                in0=products[:, :, 0, 0:HALF],
+                in1=products[:, :, 1, HALF:HEAD],
+                op=ALU.subtract,
+            )
+            nc.gpsimd.tensor_tensor(
+                out=result[:, :, HALF:HEAD],
+                in0=products[:, :, 0, HALF:HEAD],
+                in1=products[:, :, 1, 0:HALF],
+                op=ALU.add,
+            )
+            store(nc.sync, dst, sums, result)
+
+        def copy_values(g, sums):
+            dst, table = groups[g]
+            result = result_pool.tile([P, 2 * HEADS, HEAD], F32)
+            for b, (m, acc) in enumerate(sums):
+                flat = result[:, b * HEADS : (b + 1) * HEADS, :].rearrange("p h d -> p (h d)")
+                nc.scalar.copy(out=flat, in_=acc[:])
+            store(nc.scalar, dst, sums, result)
+
+        n_transposes = 2 * (N_GROUPS + 1)
+        n_matmuls = 2 * N_GROUPS
+        waiting = {}
+        for i in range(n_matmuls + LAG + 1):
+            j = i - LAG - 1
+            if 0 <= j < n_matmuls:
+                if groups[j // 2][1] is None:
+                    copy_values(j // 2, waiting[j])
+                else:
+                    norm_and_rope(j // 2, waiting[j])
+            made = []
+            if i < n_transposes:
+                made = transpose_half(i // 2, i % 2)
+                if i % 2 == 1 and i // 2 + LOADS_AHEAD <= N_GROUPS:
+                    load(i // 2 + LOADS_AHEAD)
+            j = i - LAG
+            if 0 <= j < n_matmuls:
+                waiting[j] = matmul_half(j // 2, j % 2)
+            quantise_half(i // 2, made)

@@ -36,7 +36,7 @@ def tile_qwen3attention_pa_kernel(
     with ExitStack() as ctx:
         ctx.enter_context(tc.manual_schedule())
         const = ctx.enter_context(tc.tile_pool(name="const", bufs=1))
-        raw_pool = ctx.enter_context(tc.tile_pool(name="raw", bufs=LOADS_AHEAD))
+        raw_pool = ctx.enter_context(tc.tile_pool(name="raw", bufs=2 * LOADS_AHEAD))
         grouped_pool = ctx.enter_context(tc.tile_pool(name="grouped", bufs=4))
         codes_pool = ctx.enter_context(tc.tile_pool(name="codes", bufs=3))
         small = ctx.enter_context(tc.tile_pool(name="small", bufs=4))
@@ -53,24 +53,29 @@ def tile_qwen3attention_pa_kernel(
         codes = {}
         scales = {}
 
-        def load(s):
-            raw = raw_pool.tile([P, ROW_TILES, D_MODEL], BF16)
+        def load(s, pieces=1):
             rows = sources[s].rearrange("(r p) k -> p r k", p=P)
             for half in range(2):
+                raw = raw_pool.tile([P, ROW_TILES, D_MODEL // 2], BF16)
                 features = slice(half * D_MODEL // 2, (half + 1) * D_MODEL // 2)
-                nc.sync.dma_start(out=raw[:, :, features], in_=rows[:, :, features])
-            raws[s] = raw
+                step = ROW_TILES // pieces
+                for r in range(0, ROW_TILES, step):
+                    nc.sync.dma_start(
+                        out=raw[:, r : r + step, :], in_=rows[:, r : r + step, features]
+                    )
+                raws[s, half] = raw
 
         gain_rows = const.tile([P, 2, HEAD], BF16)
         nc.vector.memset(gain_rows[:], 0.0)
         nc.sync.dma_start(out=gain_rows[0:1, 0, :], in_=q_norm_w.rearrange("(o d) -> o d", o=1))
         nc.sync.dma_start(out=gain_rows[0:1, 1, :], in_=k_norm_w.rearrange("(o d) -> o d", o=1))
-        load(0)
+        load(0, pieces=2)
+        load(1)
         cos = const.tile([P, 2, HEAD], BF16)
         sin = const.tile([P, 2, HEAD], BF16)
         nc.sync.dma_start(out=cos[:], in_=pos_cos.rearrange("(t p) d -> p t d", p=P))
         nc.sync.dma_start(out=sin[:], in_=pos_sin.rearrange("(t p) d -> p t d", p=P))
-        for s in range(1, LOADS_AHEAD):
+        for s in range(2, LOADS_AHEAD):
             load(s)
 
         ident = const.tile([P, P], F32)
@@ -129,7 +134,7 @@ def tile_qwen3attention_pa_kernel(
                 scale_bytes = pool.tile([P, PASSES, ROWS], U8, align_bytes=64)
                 codes[s] = code_words
                 scales[s] = scale_bytes
-            raw_words = raws[s][:].bitcast(F32)
+            raw_words = raws[s, half][:].bitcast(F32)
             made = []
             for c in (2 * half, 2 * half + 1):
                 grouped = grouped_pool.tile([P, 4 * ROWS], BF16, align_bytes=64)
@@ -138,7 +143,7 @@ def tile_qwen3attention_pa_kernel(
                     bank = psum_t.tile([P, 2, 2 * P], F32)
                     for u in range(2):
                         for rr in range(2):
-                            first = 2 * c * P + u
+                            first = 2 * (c % 2) * P + u
                             nc.tensor.transpose(
                                 bank[:, u, rr * P : (rr + 1) * P],
                                 raw_words[:, 2 * pair + rr, first : first + 2 * P - 1 : 2],

@@ -23,7 +23,6 @@ N_GROUPS = 8
 EPS = 1e-6
 
 LOADS_AHEAD = 4
-SHARED_SOURCES = 2
 LAG = 4
 
 FLOPS = 2 * 512 * 4096 * 2048
@@ -37,6 +36,7 @@ def tile_qwen3attention_pa_kernel(
         ctx.enter_context(tc.manual_schedule())
         const = ctx.enter_context(tc.tile_pool(name="const", bufs=1))
         raw_pool = ctx.enter_context(tc.tile_pool(name="raw", bufs=2 * LOADS_AHEAD))
+        ordered_pool = ctx.enter_context(tc.tile_pool(name="ordered", bufs=4))
         grouped_pool = ctx.enter_context(tc.tile_pool(name="grouped", bufs=4))
         codes_pool = ctx.enter_context(tc.tile_pool(name="codes", bufs=3))
         small = ctx.enter_context(tc.tile_pool(name="small", bufs=4))
@@ -127,6 +127,17 @@ def tile_qwen3attention_pa_kernel(
             for col in range(0, flat.shape[1], ROWS):
                 groups.append((flat[:, col : col + ROWS], table))
 
+        ordered = {}
+
+        def reorder_half(s, half):
+            tile = ordered_pool.tile([P, ROW_TILES, D_MODEL // PASSES], BF16)
+            raw_words = raws[s, half][:].bitcast(F32)[:, :, 2 * P : 4 * P]
+            nc.vector.tensor_copy(
+                out=tile[:].bitcast(F32).rearrange("p r (u q i) -> p r u q i", u=2, i=8),
+                in_=raw_words.rearrange("p r (q u i) -> p r u q i", u=2, i=8),
+            )
+            ordered[s, half] = tile
+
         def transpose_half(s, half):
             if half == 0:
                 pool = const if s == 0 else codes_pool
@@ -135,6 +146,7 @@ def tile_qwen3attention_pa_kernel(
                 codes[s] = code_words
                 scales[s] = scale_bytes
             raw_words = raws[s, half][:].bitcast(F32)
+            ordered_words = ordered[s, half][:].bitcast(F32)
             made = []
             for c in (2 * half, 2 * half + 1):
                 grouped = grouped_pool.tile([P, 4 * ROWS], BF16, align_bytes=64)
@@ -143,16 +155,14 @@ def tile_qwen3attention_pa_kernel(
                     bank = psum_t.tile([P, 2, 2 * P], F32)
                     for u in range(2):
                         for rr in range(2):
-                            first = 2 * (c % 2) * P + u
+                            if c % 2 == 0:
+                                words = raw_words[:, 2 * pair + rr, u : u + 2 * P - 1 : 2]
+                            else:
+                                words = ordered_words[:, 2 * pair + rr, u * P : (u + 1) * P]
                             nc.tensor.transpose(
-                                bank[:, u, rr * P : (rr + 1) * P],
-                                raw_words[:, 2 * pair + rr, first : first + 2 * P - 1 : 2],
-                                ident[:],
+                                bank[:, u, rr * P : (rr + 1) * P], words, ident[:]
                             )
-                    copy_out = nc.scalar.copy
-                    if s < SHARED_SOURCES and pair == 1:
-                        copy_out = nc.vector.tensor_copy
-                    copy_out(
+                    nc.scalar.copy(
                         out=grouped_words[:, pair * 2 * P : (pair + 1) * 2 * P, :],
                         in_=bank[:].rearrange("p u n -> p n u"),
                     )
@@ -247,6 +257,7 @@ def tile_qwen3attention_pa_kernel(
         n_transposes = 2 * (N_GROUPS + 1)
         n_matmuls = 2 * N_GROUPS
         waiting = {}
+        reorder_half(0, 0)
         for i in range(n_matmuls + LAG + 1):
             j = i - LAG - 1
             if 0 <= j < n_matmuls:
@@ -262,4 +273,8 @@ def tile_qwen3attention_pa_kernel(
             j = i - LAG
             if 0 <= j < n_matmuls:
                 waiting[j] = matmul_half(j // 2, j % 2)
+            if i == 0:
+                reorder_half(0, 1)
             quantise_half(i // 2, made)
+            if i + 2 < n_transposes:
+                reorder_half((i + 2) // 2, (i + 2) % 2)

@@ -97,6 +97,10 @@ def tile_qwen3attention_pa_kernel(
         )
         gains = const.tile([P, 2, HEAD], F32)
         nc.vector.tensor_copy(out=gains[:].rearrange("p g d -> p (g d)"), in_=acc[:, 0 : 2 * HEAD])
+        minus_gains = const.tile([P, 2, HEAD], F32)
+        nc.vector.tensor_scalar(
+            out=minus_gains[:], in0=gains[:], scalar1=-1.0, scalar2=None, op0=ALU.mult
+        )
 
         tables = []
         for kind in range(2):
@@ -116,7 +120,7 @@ def tile_qwen3attention_pa_kernel(
             nc.gpsimd.tensor_tensor(
                 out=table[:, :, 1, HALF:HEAD],
                 in0=sin[:, :, 0:HALF],
-                in1=gains[:, kind, HALF:HEAD].unsqueeze(1).to_broadcast([P, 2, HALF]),
+                in1=minus_gains[:, kind, HALF:HEAD].unsqueeze(1).to_broadcast([P, 2, HALF]),
                 op=ALU.mult,
             )
             tables.append(table)
@@ -182,8 +186,8 @@ def tile_qwen3attention_pa_kernel(
             for m in (2 * half, 2 * half + 1):
                 acc = psum_acc.tile([P, ROWS], F32)
                 sums.append((m, acc))
-            for c in range(PASSES):
-                for m, acc in sums:
+            for m, acc in sums:
+                for c in range(PASSES):
                     nc.tensor.matmul_mx(
                         out=acc[:],
                         lhsT=codes[0][:, c, m * P : (m + 1) * P].bitcast(FP8X4),
@@ -202,48 +206,79 @@ def tile_qwen3attention_pa_kernel(
                 in_=result[:].rearrange("p (b h) d -> p b (h d)", b=2),
             )
 
-        def norm_and_rope(g, sums):
+        def square_sums(sums):
+            squares = scratch.tile([P, 2, HEADS, HEAD], BF16)
+            sumsqs = []
+            for b in range(2):
+                sumsq = small.tile([P, HEADS], F32, name="sumsq%d" % b)
+                sumsqs.append(sumsq)
+            roots = []
+
+            def square(b, h):
+                nc.scalar.activation(
+                    out=squares[:, b, h, :],
+                    in_=sums[b][1][:, h * HEAD : (h + 1) * HEAD],
+                    func=ACT.Square,
+                    accum_out=sumsqs[b][:, h : h + 1],
+                )
+
+            def root(b):
+                rms = small.tile([P, HEADS], F32, name="rms%d" % b)
+                nc.scalar.activation(
+                    out=rms[:], in_=sumsqs[b][:], func=ACT.Sqrt, scale=1.0 / HEAD, bias=eps[:, 0:1]
+                )
+                roots.append(rms)
+
+            for h in range(HEADS):
+                square(0, h)
+            square(1, 0)
+            root(0)
+            for h in range(1, HEADS):
+                square(1, h)
+            root(1)
+            return roots
+
+        def norm_and_rope(g, sums, between):
             dst, table = groups[g]
-            sumsq = small.tile([P, 2 * HEADS], F32)
-            squares = scratch.tile([P, 2 * HEADS, HEAD], BF16)
-            for b, (m, acc) in enumerate(sums):
-                for h in range(HEADS):
-                    nc.scalar.activation(
-                        out=squares[:, b * HEADS + h, :],
-                        in_=acc[:, h * HEAD : (h + 1) * HEAD],
-                        func=ACT.Square,
-                        accum_out=sumsq[:, b * HEADS + h : b * HEADS + h + 1],
-                    )
-            rms = small.tile([P, 2 * HEADS], F32)
-            nc.scalar.activation(
-                out=rms[:], in_=sumsq[:], func=ACT.Sqrt, scale=1.0 / HEAD, bias=eps[:, 0:1]
-            )
-            inv_rms = small.tile([P, 2 * HEADS], F32)
-            nc.vector.reciprocal(out=inv_rms[:], in_=rms[:])
-            products = products_pool.tile([P, 2 * HEADS, 2, HEAD], F32)
-            for b, (m, acc) in enumerate(sums):
-                for h in range(HEADS):
-                    nc.vector.scalar_tensor_tensor(
-                        out=products[:, b * HEADS + h, :, :],
-                        in0=acc[:, h * HEAD : (h + 1) * HEAD].unsqueeze(1).to_broadcast([P, 2, HEAD]),
-                        scalar=inv_rms[:, b * HEADS + h : b * HEADS + h + 1],
-                        in1=table[:, m % 2, :, :],
-                        op0=ALU.mult,
-                        op1=ALU.mult,
-                    )
+            roots = square_sums(sums)
+            inverses = []
+            products = []
+            for b in range(2):
+                inv_rms = small.tile([P, HEADS], F32, name="inv%d" % b)
+                inverses.append(inv_rms)
+                product = products_pool.tile([P, HEADS, 2, HEAD], F32, name="product%d" % b)
+                products.append(product)
+
+            def multiply(b, h):
+                m, acc = sums[b]
+                nc.vector.scalar_tensor_tensor(
+                    out=products[b][:, h, :, :],
+                    in0=acc[:, h * HEAD : (h + 1) * HEAD].unsqueeze(1).to_broadcast([P, 2, HEAD]),
+                    scalar=inverses[b][:, h : h + 1],
+                    in1=table[:, m % 2, :, :],
+                    op0=ALU.mult,
+                    op1=ALU.mult,
+                )
+
+            nc.vector.reciprocal(out=inverses[0][:], in_=roots[0][:])
+            between()
+            for h in range(HEADS - 1):
+                multiply(0, h)
+            nc.vector.reciprocal(out=inverses[1][:], in_=roots[1][:])
+            multiply(0, HEADS - 1)
+            for h in range(HEADS):
+                multiply(1, h)
             result = result_pool.tile([P, 2 * HEADS, HEAD], F32)
-            nc.gpsimd.tensor_tensor(
-                out=result[:, :, 0:HALF],
-                in0=products[:, :, 0, 0:HALF],
-                in1=products[:, :, 1, HALF:HEAD],
-                op=ALU.subtract,
-            )
-            nc.gpsimd.tensor_tensor(
-                out=result[:, :, HALF:HEAD],
-                in0=products[:, :, 0, HALF:HEAD],
-                in1=products[:, :, 1, 0:HALF],
-                op=ALU.add,
-            )
+            for b in range(2):
+                halves = products[b][:].rearrange("p h k (a j) -> p h k a j", a=2)
+                nc.gpsimd.tensor_tensor(
+                    out=result[:, b * HEADS : (b + 1) * HEADS, :].rearrange(
+                        "p h (a j) -> p h a j", a=2
+                    ),
+                    in0=halves[:, :, 0, :, :],
+                    in1=halves[:, :, 1, ::-1, :],
+                    op=ALU.add,
+                )
             store(nc.sync, dst, sums, result)
 
         def copy_values(g, sums):
@@ -259,12 +294,19 @@ def tile_qwen3attention_pa_kernel(
         waiting = {}
         reorder_half(0, 0)
         for i in range(n_matmuls + LAG + 1):
+            reordered = False
+
+            def reorder_ahead():
+                if i + 1 < n_transposes and i > 0:
+                    reorder_half((i + 1) // 2, (i + 1) % 2)
+
             j = i - LAG - 1
             if 0 <= j < n_matmuls:
                 if groups[j // 2][1] is None:
                     copy_values(j // 2, waiting[j])
                 else:
-                    norm_and_rope(j // 2, waiting[j])
+                    norm_and_rope(j // 2, waiting[j], reorder_ahead)
+                    reordered = True
             made = []
             if i < n_transposes:
                 made = transpose_half(i // 2, i % 2)
@@ -275,6 +317,6 @@ def tile_qwen3attention_pa_kernel(
                 waiting[j] = matmul_half(j // 2, j % 2)
             if i == 0:
                 reorder_half(0, 1)
+            elif not reordered:
+                reorder_ahead()
             quantise_half(i // 2, made)
-            if i + 2 < n_transposes:
-                reorder_half((i + 2) // 2, (i + 2) % 2)

@@ -17,12 +17,16 @@ PASSES = 4
 HEAD = 128
 HALF = HEAD // 2
 ROWS = 512
-ROW_TILES = ROWS // P
 HEADS = ROWS // HEAD
 N_GROUPS = 8
 EPS = 1e-6
 
-LOADS_AHEAD = 4
+BLOCKS = 4
+STEPS = [(0, 0), (1, 0), (1, 1), (0, 1)] + [
+    (s, half) for s in range(2, N_GROUPS + 1) for half in range(2)
+]
+
+LOADS_AHEAD = 8
 LAG = 4
 
 FLOPS = 2 * 512 * 4096 * 2048
@@ -35,7 +39,7 @@ def tile_qwen3attention_pa_kernel(
     with ExitStack() as ctx:
         ctx.enter_context(tc.manual_schedule())
         const = ctx.enter_context(tc.tile_pool(name="const", bufs=1))
-        raw_pool = ctx.enter_context(tc.tile_pool(name="raw", bufs=2 * LOADS_AHEAD))
+        raw_pool = ctx.enter_context(tc.tile_pool(name="raw", bufs=LOADS_AHEAD))
         ordered_pool = ctx.enter_context(tc.tile_pool(name="ordered", bufs=4))
         grouped_pool = ctx.enter_context(tc.tile_pool(name="grouped", bufs=4))
         codes_pool = ctx.enter_context(tc.tile_pool(name="codes", bufs=3))
@@ -53,30 +57,36 @@ def tile_qwen3attention_pa_kernel(
         codes = {}
         scales = {}
 
-        def load(s, pieces=1):
+        def load(step):
+            s, half = STEPS[step]
+            raw = raw_pool.tile([P, BLOCKS, D_MODEL // 2], BF16)
             rows = sources[s].rearrange("(r p) k -> p r k", p=P)
-            for half in range(2):
-                raw = raw_pool.tile([P, ROW_TILES, D_MODEL // 2], BF16)
-                features = slice(half * D_MODEL // 2, (half + 1) * D_MODEL // 2)
-                step = ROW_TILES // pieces
-                for r in range(0, ROW_TILES, step):
+            if s == 0:
+                for a in range(2):
                     nc.sync.dma_start(
-                        out=raw[:, r : r + step, :], in_=rows[:, r : r + step, features]
+                        out=raw[:, 2 * a : 2 * a + 2, :],
+                        in_=rows[
+                            :, 2 * half : 2 * half + 2, a * D_MODEL // 2 : (a + 1) * D_MODEL // 2
+                        ],
                     )
-                raws[s, half] = raw
+            else:
+                nc.sync.dma_start(
+                    out=raw[:], in_=rows[:, :, half * D_MODEL // 2 : (half + 1) * D_MODEL // 2]
+                )
+            raws[step] = raw
 
         gain_rows = const.tile([P, 2, HEAD], BF16)
         nc.vector.memset(gain_rows[:], 0.0)
         nc.sync.dma_start(out=gain_rows[0:1, 0, :], in_=q_norm_w.rearrange("(o d) -> o d", o=1))
         nc.sync.dma_start(out=gain_rows[0:1, 1, :], in_=k_norm_w.rearrange("(o d) -> o d", o=1))
-        load(0, pieces=2)
-        load(1)
+        for step in range(4):
+            load(step)
         cos = const.tile([P, 2, HEAD], BF16)
         sin = const.tile([P, 2, HEAD], BF16)
         nc.sync.dma_start(out=cos[:], in_=pos_cos.rearrange("(t p) d -> p t d", p=P))
         nc.sync.dma_start(out=sin[:], in_=pos_sin.rearrange("(t p) d -> p t d", p=P))
-        for s in range(2, LOADS_AHEAD):
-            load(s)
+        for step in range(4, LOADS_AHEAD):
+            load(step)
 
         ident = const.tile([P, P], F32)
         make_identity(nc, ident[:])
@@ -97,10 +107,6 @@ def tile_qwen3attention_pa_kernel(
         )
         gains = const.tile([P, 2, HEAD], F32)
         nc.vector.tensor_copy(out=gains[:].rearrange("p g d -> p (g d)"), in_=acc[:, 0 : 2 * HEAD])
-        minus_gains = const.tile([P, 2, HEAD], F32)
-        nc.vector.tensor_scalar(
-            out=minus_gains[:], in0=gains[:], scalar1=-1.0, scalar2=None, op0=ALU.mult
-        )
 
         tables = []
         for kind in range(2):
@@ -120,7 +126,7 @@ def tile_qwen3attention_pa_kernel(
             nc.gpsimd.tensor_tensor(
                 out=table[:, :, 1, HALF:HEAD],
                 in0=sin[:, :, 0:HALF],
-                in1=minus_gains[:, kind, HALF:HEAD].unsqueeze(1).to_broadcast([P, 2, HALF]),
+                in1=gains[:, kind, HALF:HEAD].unsqueeze(1).to_broadcast([P, 2, HALF]),
                 op=ALU.mult,
             )
             tables.append(table)
@@ -133,51 +139,58 @@ def tile_qwen3attention_pa_kernel(
 
         ordered = {}
 
-        def reorder_half(s, half):
-            tile = ordered_pool.tile([P, ROW_TILES, D_MODEL // PASSES], BF16)
-            raw_words = raws[s, half][:].bitcast(F32)[:, :, 2 * P : 4 * P]
-            nc.vector.tensor_copy(
-                out=tile[:].bitcast(F32).rearrange("p r (u q i) -> p r u q i", u=2, i=8),
-                in_=raw_words.rearrange("p r (q u i) -> p r u q i", u=2, i=8),
-            )
-            ordered[s, half] = tile
+        def reorder(step):
+            tile = ordered_pool.tile([P, BLOCKS, 2 * P], F32)
+            raw_words = raws[step][:].bitcast(F32)
+            height = BLOCKS // 2 if STEPS[step][0] == 0 else BLOCKS
+            for first in range(0, BLOCKS, height):
+                blocks = slice(first, first + height)
+                nc.vector.tensor_copy(
+                    out=tile[:, blocks, :].rearrange("p k (u q i) -> p k u q i", u=2, i=8),
+                    in_=raw_words[:, blocks, 2 * P : 4 * P].rearrange(
+                        "p k (q u i) -> p k u q i", u=2, i=8
+                    ),
+                )
+            ordered[step] = tile
 
-        def transpose_half(s, half):
+        def transpose(step):
+            s, half = STEPS[step]
             if half == 0:
                 pool = const if s == 0 else codes_pool
                 code_words = pool.tile([P, PASSES, ROWS], U32, align_bytes=64)
                 scale_bytes = pool.tile([P, PASSES, ROWS], U8, align_bytes=64)
                 codes[s] = code_words
                 scales[s] = scale_bytes
-            raw_words = raws[s, half][:].bitcast(F32)
-            ordered_words = ordered[s, half][:].bitcast(F32)
+            raw_words = raws[step][:].bitcast(F32)
             made = []
-            for c in (2 * half, 2 * half + 1):
+            for g in range(2):
                 grouped = grouped_pool.tile([P, 4 * ROWS], BF16, align_bytes=64)
                 grouped_words = grouped[:].bitcast(F32).rearrange("p (n u) -> p n u", u=2)
-                for pair in range(ROW_TILES // 2):
+                for part in range(2):
+                    odd, first = (part, 2 * g) if s == 0 else (g, 2 * part)
                     bank = psum_t.tile([P, 2, 2 * P], F32)
                     for u in range(2):
                         for rr in range(2):
-                            if c % 2 == 0:
-                                words = raw_words[:, 2 * pair + rr, u : u + 2 * P - 1 : 2]
+                            if odd:
+                                words = ordered[step][:, first + rr, u * P : (u + 1) * P]
                             else:
-                                words = ordered_words[:, 2 * pair + rr, u * P : (u + 1) * P]
+                                words = raw_words[:, first + rr, u : u + 2 * P - 1 : 2]
                             nc.tensor.transpose(
                                 bank[:, u, rr * P : (rr + 1) * P], words, ident[:]
                             )
                     nc.scalar.copy(
-                        out=grouped_words[:, pair * 2 * P : (pair + 1) * 2 * P, :],
+                        out=grouped_words[:, part * 2 * P : (part + 1) * 2 * P, :],
                         in_=bank[:].rearrange("p u n -> p n u"),
                     )
-                made.append((c, grouped))
+                made.append(grouped)
             return made
 
-        def quantise_half(s, made):
-            for c, grouped in made:
+        def quantise(step, made):
+            s, half = STEPS[step]
+            for g, grouped in enumerate(made):
                 nc.vector.quantize_mx(
-                    out=codes[s][:, c, :].bitcast(FP8X4),
-                    scales=scales[s][:, c, :],
+                    out=codes[s][:, 2 * half + g, :].bitcast(FP8X4),
+                    scales=scales[s][:, 2 * half + g, :],
                     in_=grouped[:],
                 )
 
@@ -186,12 +199,14 @@ def tile_qwen3attention_pa_kernel(
             for m in (2 * half, 2 * half + 1):
                 acc = psum_acc.tile([P, ROWS], F32)
                 sums.append((m, acc))
-            for m, acc in sums:
-                for c in range(PASSES):
+            for c in range(PASSES):
+                for m, acc in sums:
+                    row = 2 * half + c // 2
+                    first = (2 * (c % 2) + m % 2) * P
                     nc.tensor.matmul_mx(
                         out=acc[:],
-                        lhsT=codes[0][:, c, m * P : (m + 1) * P].bitcast(FP8X4),
-                        lhsT_scale=scales[0][:, c, m * P : (m + 1) * P],
+                        lhsT=codes[0][:, row, first : first + P].bitcast(FP8X4),
+                        lhsT_scale=scales[0][:, row, first : first + P],
                         rhs=codes[g + 1][:, c, :].bitcast(FP8X4),
                         rhs_scale=scales[g + 1][:, c, :],
                         start=(c == 0),
@@ -242,17 +257,15 @@ def tile_qwen3attention_pa_kernel(
             dst, table = groups[g]
             roots = square_sums(sums)
             inverses = []
-            products = []
+            products = products_pool.tile([P, 2 * HEADS, 2, HEAD], F32)
             for b in range(2):
                 inv_rms = small.tile([P, HEADS], F32, name="inv%d" % b)
                 inverses.append(inv_rms)
-                product = products_pool.tile([P, HEADS, 2, HEAD], F32, name="product%d" % b)
-                products.append(product)
 
             def multiply(b, h):
                 m, acc = sums[b]
                 nc.vector.scalar_tensor_tensor(
-                    out=products[b][:, h, :, :],
+                    out=products[:, b * HEADS + h, :, :],
                     in0=acc[:, h * HEAD : (h + 1) * HEAD].unsqueeze(1).to_broadcast([P, 2, HEAD]),
                     scalar=inverses[b][:, h : h + 1],
                     in1=table[:, m % 2, :, :],
@@ -269,16 +282,18 @@ def tile_qwen3attention_pa_kernel(
             for h in range(HEADS):
                 multiply(1, h)
             result = result_pool.tile([P, 2 * HEADS, HEAD], F32)
-            for b in range(2):
-                halves = products[b][:].rearrange("p h k (a j) -> p h k a j", a=2)
-                nc.gpsimd.tensor_tensor(
-                    out=result[:, b * HEADS : (b + 1) * HEADS, :].rearrange(
-                        "p h (a j) -> p h a j", a=2
-                    ),
-                    in0=halves[:, :, 0, :, :],
-                    in1=halves[:, :, 1, ::-1, :],
-                    op=ALU.add,
-                )
+            nc.gpsimd.tensor_tensor(
+                out=result[:, :, 0:HALF],
+                in0=products[:, :, 0, 0:HALF],
+                in1=products[:, :, 1, HALF:HEAD],
+                op=ALU.subtract,
+            )
+            nc.gpsimd.tensor_tensor(
+                out=result[:, :, HALF:HEAD],
+                in0=products[:, :, 0, HALF:HEAD],
+                in1=products[:, :, 1, 0:HALF],
+                op=ALU.add,
+            )
             store(nc.sync, dst, sums, result)
 
         def copy_values(g, sums):
@@ -289,34 +304,34 @@ def tile_qwen3attention_pa_kernel(
                 nc.scalar.copy(out=flat, in_=acc[:])
             store(nc.scalar, dst, sums, result)
 
-        n_transposes = 2 * (N_GROUPS + 1)
         n_matmuls = 2 * N_GROUPS
+        sums_at = {}
+        for j in range(n_matmuls):
+            sums_at[j + LAG - 1 if j < 2 else j + LAG] = j
         waiting = {}
-        reorder_half(0, 0)
+        reorder(0)
         for i in range(n_matmuls + LAG + 1):
+            def reorder_next():
+                if i + 1 < len(STEPS):
+                    reorder(i + 1)
+
             reordered = False
-
-            def reorder_ahead():
-                if i + 1 < n_transposes and i > 0:
-                    reorder_half((i + 1) // 2, (i + 1) % 2)
-
-            j = i - LAG - 1
-            if 0 <= j < n_matmuls:
+            if i - 1 in sums_at:
+                j = sums_at[i - 1]
                 if groups[j // 2][1] is None:
                     copy_values(j // 2, waiting[j])
                 else:
-                    norm_and_rope(j // 2, waiting[j], reorder_ahead)
+                    norm_and_rope(j // 2, waiting[j], reorder_next)
                     reordered = True
             made = []
-            if i < n_transposes:
-                made = transpose_half(i // 2, i % 2)
-                if i % 2 == 1 and i // 2 + LOADS_AHEAD <= N_GROUPS:
-                    load(i // 2 + LOADS_AHEAD)
-            j = i - LAG
-            if 0 <= j < n_matmuls:
+            if i < len(STEPS):
+                made = transpose(i)
+                if i + LOADS_AHEAD < len(STEPS):
+                    load(i + LOADS_AHEAD)
+            if i in sums_at:
+                j = sums_at[i]
                 waiting[j] = matmul_half(j // 2, j % 2)
-            if i == 0:
-                reorder_half(0, 1)
-            elif not reordered:
-                reorder_ahead()
-            quantise_half(i // 2, made)
+            if not reordered:
+                reorder_next()
+            if i < len(STEPS):
+                quantise(i, made)

@@ -93,7 +93,7 @@ def tile_qwen3attention_pa_kernel(
         eps = const.tile([P, 1], F32)
         nc.vector.memset(eps[:], EPS)
         warm = const.tile([P, 1], F32)
-        nc.scalar.activation(out=warm[:], in_=eps[:], func=ACT.Sqrt)
+        nc.scalar.activation(out=warm[:], in_=eps[:], func=ACT.Abs_reciprocal_sqrt)
 
         ones = const.tile([P, P], BF16)
         nc.vector.memset(ones[:], 1.0)
@@ -153,7 +153,7 @@ def tile_qwen3attention_pa_kernel(
                 )
             ordered[step] = tile
 
-        def transpose(step):
+        def transpose(step, between):
             s, half = STEPS[step]
             if half == 0:
                 pool = const if s == 0 else codes_pool
@@ -165,24 +165,28 @@ def tile_qwen3attention_pa_kernel(
             made = []
             for g in range(2):
                 grouped = grouped_pool.tile([P, 4 * ROWS], BF16, align_bytes=64)
-                grouped_words = grouped[:].bitcast(F32).rearrange("p (n u) -> p n u", u=2)
-                for part in range(2):
-                    odd, first = (part, 2 * g) if s == 0 else (g, 2 * part)
+                made.append(grouped)
+            for first_half in range(2):
+                for second_half in range(2):
+                    odd = first_half
+                    g, part = (second_half, odd) if s == 0 else (odd, second_half)
                     bank = psum_t.tile([P, 2, 2 * P], F32)
                     for u in range(2):
                         for rr in range(2):
+                            block = 2 * second_half + rr
                             if odd:
-                                words = ordered[step][:, first + rr, u * P : (u + 1) * P]
+                                words = ordered[step][:, block, u * P : (u + 1) * P]
                             else:
-                                words = raw_words[:, first + rr, u : u + 2 * P - 1 : 2]
+                                words = raw_words[:, block, u : u + 2 * P - 1 : 2]
                             nc.tensor.transpose(
                                 bank[:, u, rr * P : (rr + 1) * P], words, ident[:]
                             )
+                    grouped_words = made[g][:].bitcast(F32).rearrange("p (n u) -> p n u", u=2)
                     nc.scalar.copy(
                         out=grouped_words[:, part * 2 * P : (part + 1) * 2 * P, :],
                         in_=bank[:].rearrange("p u n -> p n u"),
                     )
-                made.append(grouped)
+                between(odd)
             return made
 
         def quantise(step, made):
@@ -194,12 +198,15 @@ def tile_qwen3attention_pa_kernel(
                     in_=grouped[:],
                 )
 
-        def matmul_half(g, half):
+        def open_sums(half):
             sums = []
             for m in (2 * half, 2 * half + 1):
                 acc = psum_acc.tile([P, ROWS], F32)
                 sums.append((m, acc))
-            for c in range(PASSES):
+            return sums
+
+        def matmul_passes(g, half, sums, passes):
+            for c in passes:
                 for m, acc in sums:
                     row = 2 * half + c // 2
                     first = (2 * (c % 2) + m % 2) * P
@@ -212,11 +219,10 @@ def tile_qwen3attention_pa_kernel(
                         start=(c == 0),
                         stop=(c == PASSES - 1),
                     )
-            return sums
 
-        def store(queue, dst, sums, result):
+        def store(dst, sums, result):
             first = sums[0][0] * P
-            queue.dma_start(
+            nc.sync.dma_start(
                 out=dst[first : first + 2 * P, :].rearrange("(b p) f -> p b f", p=P),
                 in_=result[:].rearrange("p (b h) d -> p b (h d)", b=2),
             )
@@ -227,7 +233,7 @@ def tile_qwen3attention_pa_kernel(
             for b in range(2):
                 sumsq = small.tile([P, HEADS], F32, name="sumsq%d" % b)
                 sumsqs.append(sumsq)
-            roots = []
+            inverses = []
 
             def square(b, h):
                 nc.scalar.activation(
@@ -237,30 +243,30 @@ def tile_qwen3attention_pa_kernel(
                     accum_out=sumsqs[b][:, h : h + 1],
                 )
 
-            def root(b):
-                rms = small.tile([P, HEADS], F32, name="rms%d" % b)
+            def inverse_root(b):
+                inv_rms = small.tile([P, HEADS], F32, name="inv%d" % b)
                 nc.scalar.activation(
-                    out=rms[:], in_=sumsqs[b][:], func=ACT.Sqrt, scale=1.0 / HEAD, bias=eps[:, 0:1]
+                    out=inv_rms[:],
+                    in_=sumsqs[b][:],
+                    func=ACT.Abs_reciprocal_sqrt,
+                    scale=1.0 / HEAD,
+                    bias=eps[:, 0:1],
                 )
-                roots.append(rms)
+                inverses.append(inv_rms)
 
             for h in range(HEADS):
                 square(0, h)
             square(1, 0)
-            root(0)
+            inverse_root(0)
             for h in range(1, HEADS):
                 square(1, h)
-            root(1)
-            return roots
+            inverse_root(1)
+            return inverses
 
         def norm_and_rope(g, sums, between):
             dst, table = groups[g]
-            roots = square_sums(sums)
-            inverses = []
+            inverses = square_sums(sums)
             products = products_pool.tile([P, 2 * HEADS, 2, HEAD], F32)
-            for b in range(2):
-                inv_rms = small.tile([P, HEADS], F32, name="inv%d" % b)
-                inverses.append(inv_rms)
 
             def multiply(b, h):
                 m, acc = sums[b]
@@ -273,14 +279,10 @@ def tile_qwen3attention_pa_kernel(
                     op1=ALU.mult,
                 )
 
-            nc.vector.reciprocal(out=inverses[0][:], in_=roots[0][:])
             between()
-            for h in range(HEADS - 1):
-                multiply(0, h)
-            nc.vector.reciprocal(out=inverses[1][:], in_=roots[1][:])
-            multiply(0, HEADS - 1)
-            for h in range(HEADS):
-                multiply(1, h)
+            for b in range(2):
+                for h in range(HEADS):
+                    multiply(b, h)
             result = result_pool.tile([P, 2 * HEADS, HEAD], F32)
             nc.gpsimd.tensor_tensor(
                 out=result[:, :, 0:HALF],
@@ -294,15 +296,19 @@ def tile_qwen3attention_pa_kernel(
                 in1=products[:, :, 1, 0:HALF],
                 op=ALU.add,
             )
-            store(nc.sync, dst, sums, result)
+            store(dst, sums, result)
 
         def copy_values(g, sums):
             dst, table = groups[g]
             result = result_pool.tile([P, 2 * HEADS, HEAD], F32)
-            for b, (m, acc) in enumerate(sums):
+            for b, copy_out, queue in (
+                (0, nc.scalar.copy, nc.scalar),
+                (1, nc.vector.tensor_copy, nc.sync),
+            ):
+                m, acc = sums[b]
                 flat = result[:, b * HEADS : (b + 1) * HEADS, :].rearrange("p h d -> p (h d)")
-                nc.scalar.copy(out=flat, in_=acc[:])
-            store(nc.scalar, dst, sums, result)
+                copy_out(out=flat, in_=acc[:])
+                queue.dma_start(out=dst[m * P : (m + 1) * P, :], in_=flat)
 
         n_matmuls = 2 * N_GROUPS
         sums_at = {}
@@ -323,14 +329,24 @@ def tile_qwen3attention_pa_kernel(
                 else:
                     norm_and_rope(j // 2, waiting[j], reorder_next)
                     reordered = True
-            made = []
-            if i < len(STEPS):
-                made = transpose(i)
-                if i + LOADS_AHEAD < len(STEPS):
-                    load(i + LOADS_AHEAD)
+            sums = []
             if i in sums_at:
                 j = sums_at[i]
-                waiting[j] = matmul_half(j // 2, j % 2)
+                sums = open_sums(j % 2)
+                waiting[j] = sums
+
+            def passes(odd):
+                if sums:
+                    matmul_passes(j // 2, j % 2, sums, (2 * odd, 2 * odd + 1))
+
+            made = []
+            if i < len(STEPS):
+                made = transpose(i, passes)
+                if i + LOADS_AHEAD < len(STEPS):
+                    load(i + LOADS_AHEAD)
+            else:
+                passes(0)
+                passes(1)
             if not reordered:
                 reorder_next()
             if i < len(STEPS):

@@ -186,7 +186,7 @@ def tile_qwen3attention_pa_kernel(
                         out=grouped_words[:, part * 2 * P : (part + 1) * 2 * P, :],
                         in_=bank[:].rearrange("p u n -> p n u"),
                     )
-                between(odd)
+                    between(2 * first_half + second_half)
             return made
 
         def quantise(step, made):
@@ -228,44 +228,28 @@ def tile_qwen3attention_pa_kernel(
             )
 
         def square_sums(sums):
-            squares = scratch.tile([P, 2, HEADS, HEAD], BF16)
-            sumsqs = []
-            for b in range(2):
-                sumsq = small.tile([P, HEADS], F32, name="sumsq%d" % b)
-                sumsqs.append(sumsq)
-            inverses = []
+            squares = scratch.tile([P, 2 * HEADS, HEAD], BF16)
+            sumsq = small.tile([P, 2 * HEADS], F32)
+            for b, (m, acc) in enumerate(sums):
+                for h in range(HEADS):
+                    nc.scalar.activation(
+                        out=squares[:, b * HEADS + h, :],
+                        in_=acc[:, h * HEAD : (h + 1) * HEAD],
+                        func=ACT.Square,
+                        accum_out=sumsq[:, b * HEADS + h : b * HEADS + h + 1],
+                    )
+            return sumsq
 
-            def square(b, h):
-                nc.scalar.activation(
-                    out=squares[:, b, h, :],
-                    in_=sums[b][1][:, h * HEAD : (h + 1) * HEAD],
-                    func=ACT.Square,
-                    accum_out=sumsqs[b][:, h : h + 1],
-                )
-
-            def inverse_root(b):
-                inv_rms = small.tile([P, HEADS], F32, name="inv%d" % b)
-                nc.scalar.activation(
-                    out=inv_rms[:],
-                    in_=sumsqs[b][:],
-                    func=ACT.Abs_reciprocal_sqrt,
-                    scale=1.0 / HEAD,
-                    bias=eps[:, 0:1],
-                )
-                inverses.append(inv_rms)
-
-            for h in range(HEADS):
-                square(0, h)
-            square(1, 0)
-            inverse_root(0)
-            for h in range(1, HEADS):
-                square(1, h)
-            inverse_root(1)
-            return inverses
-
-        def norm_and_rope(g, sums, between):
+        def norm_and_rope(g, sums, sumsq, between):
             dst, table = groups[g]
-            inverses = square_sums(sums)
+            inv_rms = small.tile([P, 2 * HEADS], F32)
+            nc.scalar.activation(
+                out=inv_rms[:],
+                in_=sumsq[:],
+                func=ACT.Abs_reciprocal_sqrt,
+                scale=1.0 / HEAD,
+                bias=eps[:, 0:1],
+            )
             products = products_pool.tile([P, 2 * HEADS, 2, HEAD], F32)
 
             def multiply(b, h):
@@ -273,7 +257,7 @@ def tile_qwen3attention_pa_kernel(
                 nc.vector.scalar_tensor_tensor(
                     out=products[:, b * HEADS + h, :, :],
                     in0=acc[:, h * HEAD : (h + 1) * HEAD].unsqueeze(1).to_broadcast([P, 2, HEAD]),
-                    scalar=inverses[b][:, h : h + 1],
+                    scalar=inv_rms[:, b * HEADS + h : b * HEADS + h + 1],
                     in1=table[:, m % 2, :, :],
                     op0=ALU.mult,
                     op1=ALU.mult,
@@ -321,33 +305,35 @@ def tile_qwen3attention_pa_kernel(
                 if i + 1 < len(STEPS):
                     reorder(i + 1)
 
-            reordered = False
-            if i - 1 in sums_at:
-                j = sums_at[i - 1]
-                if groups[j // 2][1] is None:
-                    copy_values(j // 2, waiting[j])
+            done = sums_at.get(i - 1)
+            sumsq = None
+            if done is not None:
+                if groups[done // 2][1] is None:
+                    copy_values(done // 2, waiting[done])
                 else:
-                    norm_and_rope(j // 2, waiting[j], reorder_next)
-                    reordered = True
+                    sumsq = square_sums(waiting[done])
+            j = sums_at.get(i)
             sums = []
-            if i in sums_at:
-                j = sums_at[i]
+            if j is not None:
                 sums = open_sums(j % 2)
                 waiting[j] = sums
 
-            def passes(odd):
-                if sums:
-                    matmul_passes(j // 2, j % 2, sums, (2 * odd, 2 * odd + 1))
+            def after_bank(n):
+                if n == 0:
+                    if sumsq is not None:
+                        norm_and_rope(done // 2, waiting[done], sumsq, reorder_next)
+                    else:
+                        reorder_next()
+                if n % 2 == 1 and sums:
+                    matmul_passes(j // 2, j % 2, sums, (n - 1, n))
 
             made = []
             if i < len(STEPS):
-                made = transpose(i, passes)
+                made = transpose(i, after_bank)
                 if i + LOADS_AHEAD < len(STEPS):
                     load(i + LOADS_AHEAD)
             else:
-                passes(0)
-                passes(1)
-            if not reordered:
-                reorder_next()
+                for n in range(4):
+                    after_bank(n)
             if i < len(STEPS):
                 quantise(i, made)

@@ -45,7 +45,7 @@ def tile_qwen3attention_pa_kernel(
         codes_pool = ctx.enter_context(tc.tile_pool(name="codes", bufs=3))
         small = ctx.enter_context(tc.tile_pool(name="small", bufs=4))
         scratch = ctx.enter_context(tc.tile_pool(name="scratch", bufs=2))
-        products_pool = ctx.enter_context(tc.tile_pool(name="products", bufs=5))
+        products_pool = ctx.enter_context(tc.tile_pool(name="products", bufs=7))
         result_pool = ctx.enter_context(tc.tile_pool(name="result", bufs=5))
         psum_t = ctx.enter_context(tc.psum_pool(name="psum_t", bufs=4))
         psum_acc = ctx.enter_context(tc.psum_pool(name="psum_acc", bufs=4))
@@ -140,17 +140,18 @@ def tile_qwen3attention_pa_kernel(
         ordered = {}
 
         def reorder(step):
+            s, half = STEPS[step]
+            if s > 0 and half == 1:
+                return
             tile = ordered_pool.tile([P, BLOCKS, 2 * P], F32)
             raw_words = raws[step][:].bitcast(F32)
-            height = BLOCKS // 2 if STEPS[step][0] == 0 else BLOCKS
-            for first in range(0, BLOCKS, height):
-                blocks = slice(first, first + height)
-                nc.vector.tensor_copy(
-                    out=tile[:, blocks, :].rearrange("p k (u q i) -> p k u q i", u=2, i=8),
-                    in_=raw_words[:, blocks, 2 * P : 4 * P].rearrange(
-                        "p k (q u i) -> p k u q i", u=2, i=8
-                    ),
-                )
+            blocks = slice(0, BLOCKS // 2 if s == 0 else BLOCKS)
+            nc.vector.tensor_copy(
+                out=tile[:, blocks, :].rearrange("p k (u q i) -> p k u q i", u=2, i=8),
+                in_=raw_words[:, blocks, 2 * P : 4 * P].rearrange(
+                    "p k (q u i) -> p k u q i", u=2, i=8
+                ),
+            )
             ordered[step] = tile
 
         def transpose(step, between):
@@ -174,10 +175,11 @@ def tile_qwen3attention_pa_kernel(
                     for u in range(2):
                         for rr in range(2):
                             block = 2 * second_half + rr
-                            if odd:
+                            if odd and not (half if s > 0 else second_half):
                                 words = ordered[step][:, block, u * P : (u + 1) * P]
                             else:
-                                words = raw_words[:, block, u : u + 2 * P - 1 : 2]
+                                start = 2 * odd * P + u
+                                words = raw_words[:, block, start : start + 2 * P - 1 : 2]
                             nc.tensor.transpose(
                                 bank[:, u, rr * P : (rr + 1) * P], words, ident[:]
                             )
@@ -295,9 +297,9 @@ def tile_qwen3attention_pa_kernel(
                 queue.dma_start(out=dst[m * P : (m + 1) * P, :], in_=flat)
 
         n_matmuls = 2 * N_GROUPS
-        sums_at = {}
-        for j in range(n_matmuls):
-            sums_at[j + LAG - 1 if j < 2 else j + LAG] = j
+        plan = {LAG - 1: (0, (0, 1, 2, 3)), LAG: (1, (0, 1)), LAG + 1: (1, (2, 3))}
+        for j in range(2, n_matmuls):
+            plan[j + LAG] = (j, (0, 1, 2, 3))
         waiting = {}
         reorder(0)
         for i in range(n_matmuls + LAG + 1):
@@ -305,18 +307,16 @@ def tile_qwen3attention_pa_kernel(
                 if i + 1 < len(STEPS):
                     reorder(i + 1)
 
-            done = sums_at.get(i - 1)
+            done, passes = plan.get(i - 1, (None, ()))
             sumsq = None
-            if done is not None:
+            if PASSES - 1 in passes:
                 if groups[done // 2][1] is None:
                     copy_values(done // 2, waiting[done])
                 else:
                     sumsq = square_sums(waiting[done])
-            j = sums_at.get(i)
-            sums = []
-            if j is not None:
-                sums = open_sums(j % 2)
-                waiting[j] = sums
+            j, passes = plan.get(i, (None, ()))
+            if 0 in passes:
+                waiting[j] = open_sums(j % 2)
 
             def after_bank(n):
                 if n == 0:
@@ -324,8 +324,8 @@ def tile_qwen3attention_pa_kernel(
                         norm_and_rope(done // 2, waiting[done], sumsq, reorder_next)
                     else:
                         reorder_next()
-                if n % 2 == 1 and sums:
-                    matmul_passes(j // 2, j % 2, sums, (n - 1, n))
+                if n == 3 and passes:
+                    matmul_passes(j // 2, j % 2, waiting[j], passes)
 
             made = []
             if i < len(STEPS):

from contextlib import ExitStack

import concourse.mybir as mybir
from concourse.masks import make_identity

F32 = mybir.dt.float32
BF16 = mybir.dt.bfloat16
U32 = mybir.dt.uint32
U8 = mybir.dt.uint8
FP8X4 = mybir.dt.float8_e4m3fn_x4
ACT = mybir.ActivationFunctionType
ALU = mybir.AluOpType

P = 128
D_MODEL = 2048
PASSES = 4
HEAD = 128
HALF = HEAD // 2
ROWS = 512
HEADS = ROWS // HEAD
N_GROUPS = 8
EPS = 1e-6

BLOCKS = 4
STEPS = [(0, 0), (1, 0), (1, 1), (0, 1)] + [
    (s, half) for s in range(2, N_GROUPS + 1) for half in range(2)
]

LOADS_AHEAD = 8
LAG = 4

FLOPS = 2 * 512 * 4096 * 2048


def tile_qwen3attention_pa_kernel(
    tc, x, pos_cos, pos_sin, w_qkv, q_norm_w, k_norm_w, out_0, out_1, out_2
):
    nc = tc.nc
    with ExitStack() as ctx:
        ctx.enter_context(tc.manual_schedule())
        const = ctx.enter_context(tc.tile_pool(name="const", bufs=1))
        raw_pool = ctx.enter_context(tc.tile_pool(name="raw", bufs=LOADS_AHEAD))
        ordered_pool = ctx.enter_context(tc.tile_pool(name="ordered", bufs=4))
        grouped_pool = ctx.enter_context(tc.tile_pool(name="grouped", bufs=4))
        codes_pool = ctx.enter_context(tc.tile_pool(name="codes", bufs=3))
        small = ctx.enter_context(tc.tile_pool(name="small", bufs=4))
        scratch = ctx.enter_context(tc.tile_pool(name="scratch", bufs=2))
        products_pool = ctx.enter_context(tc.tile_pool(name="products", bufs=7))
        result_pool = ctx.enter_context(tc.tile_pool(name="result", bufs=5))
        psum_t = ctx.enter_context(tc.psum_pool(name="psum_t", bufs=4))
        psum_acc = ctx.enter_context(tc.psum_pool(name="psum_acc", bufs=4))

        sources = [x.rearrange("b s d -> (b s) d")]
        for g in range(N_GROUPS):
            sources.append(w_qkv[g * ROWS : (g + 1) * ROWS, :])
        raws = {}
        codes = {}
        scales = {}

        def load(step):
            s, half = STEPS[step]
            raw = raw_pool.tile([P, BLOCKS, D_MODEL // 2], BF16)
            rows = sources[s].rearrange("(r p) k -> p r k", p=P)
            if s == 0:
                for a in range(2):
                    nc.sync.dma_start(
                        out=raw[:, 2 * a : 2 * a + 2, :],
                        in_=rows[
                            :, 2 * half : 2 * half + 2, a * D_MODEL // 2 : (a + 1) * D_MODEL // 2
                        ],
                    )
            else:
                nc.sync.dma_start(
                    out=raw[:], in_=rows[:, :, half * D_MODEL // 2 : (half + 1) * D_MODEL // 2]
                )
            raws[step] = raw

        gain_rows = const.tile([P, 2, HEAD], BF16)
        nc.vector.memset(gain_rows[:], 0.0)
        nc.sync.dma_start(out=gain_rows[0:1, 0, :], in_=q_norm_w.rearrange("(o d) -> o d", o=1))
        nc.sync.dma_start(out=gain_rows[0:1, 1, :], in_=k_norm_w.rearrange("(o d) -> o d", o=1))
        for step in range(4):
            load(step)
        cos = const.tile([P, 2, HEAD], BF16)
        sin = const.tile([P, 2, HEAD], BF16)
        nc.sync.dma_start(out=cos[:], in_=pos_cos.rearrange("(t p) d -> p t d", p=P))
        nc.sync.dma_start(out=sin[:], in_=pos_sin.rearrange("(t p) d -> p t d", p=P))
        for step in range(4, LOADS_AHEAD):
            load(step)

        ident = const.tile([P, P], F32)
        make_identity(nc, ident[:])
        eps = const.tile([P, 1], F32)
        nc.vector.memset(eps[:], EPS)
        warm = const.tile([P, 1], F32)
        nc.scalar.activation(out=warm[:], in_=eps[:], func=ACT.Abs_reciprocal_sqrt)

        ones = const.tile([P, P], BF16)
        nc.vector.memset(ones[:], 1.0)
        acc = psum_acc.tile([P, ROWS], F32)
        nc.tensor.matmul(
            out=acc[:, 0 : 2 * HEAD],
            lhsT=ones[:],
            rhs=gain_rows[:].rearrange("p g d -> p (g d)"),
            start=True,
            stop=True,
        )
        gains = const.tile([P, 2, HEAD], F32)
        nc.vector.tensor_copy(out=gains[:].rearrange("p g d -> p (g d)"), in_=acc[:, 0 : 2 * HEAD])

        tables = []
        for kind in range(2):
            table = const.tile([P, 2, 2, HEAD], F32, name="table%d" % kind)
            nc.gpsimd.tensor_tensor(
                out=table[:, :, 0, :],
                in0=cos[:],
                in1=gains[:, kind, :].unsqueeze(1).to_broadcast([P, 2, HEAD]),
                op=ALU.mult,
            )
            nc.gpsimd.tensor_tensor(
                out=table[:, :, 1, 0:HALF],
                in0=sin[:, :, HALF:HEAD],
                in1=gains[:, kind, 0:HALF].unsqueeze(1).to_broadcast([P, 2, HALF]),
                op=ALU.mult,
            )
            nc.gpsimd.tensor_tensor(
                out=table[:, :, 1, HALF:HEAD],
                in0=sin[:, :, 0:HALF],
                in1=gains[:, kind, HALF:HEAD].unsqueeze(1).to_broadcast([P, 2, HALF]),
                op=ALU.mult,
            )
            tables.append(table)

        groups = []
        for out, table in ((out_0, tables[0]), (out_1, tables[1]), (out_2, None)):
            flat = out.rearrange("b s h d -> (b s) (h d)")
            for col in range(0, flat.shape[1], ROWS):
                groups.append((flat[:, col : col + ROWS], table))

        ordered = {}

        def reorder(step):
            s, half = STEPS[step]
            if s > 0 and half == 1:
                return
            tile = ordered_pool.tile([P, BLOCKS, 2 * P], F32)
            raw_words = raws[step][:].bitcast(F32)
            blocks = slice(0, BLOCKS // 2 if s == 0 else BLOCKS)
            nc.vector.tensor_copy(
                out=tile[:, blocks, :].rearrange("p k (u q i) -> p k u q i", u=2, i=8),
                in_=raw_words[:, blocks, 2 * P : 4 * P].rearrange(
                    "p k (q u i) -> p k u q i", u=2, i=8
                ),
            )
            ordered[step] = tile

        def transpose(step, between):
            s, half = STEPS[step]
            if half == 0:
                pool = const if s == 0 else codes_pool
                code_words = pool.tile([P, PASSES, ROWS], U32, align_bytes=64)
                scale_bytes = pool.tile([P, PASSES, ROWS], U8, align_bytes=64)
                codes[s] = code_words
                scales[s] = scale_bytes
            raw_words = raws[step][:].bitcast(F32)
            made = []
            for g in range(2):
                grouped = grouped_pool.tile([P, 4 * ROWS], BF16, align_bytes=64)
                made.append(grouped)
            for first_half in range(2):
                for second_half in range(2):
                    odd = first_half
                    g, part = (second_half, odd) if s == 0 else (odd, second_half)
                    bank = psum_t.tile([P, 2, 2 * P], F32)
                    for u in range(2):
                        for rr in range(2):
                            block = 2 * second_half + rr
                            if odd and not (half if s > 0 else second_half):
                                words = ordered[step][:, block, u * P : (u + 1) * P]
                            else:
                                start = 2 * odd * P + u
                                words = raw_words[:, block, start : start + 2 * P - 1 : 2]
                            nc.tensor.transpose(
                                bank[:, u, rr * P : (rr + 1) * P], words, ident[:]
                            )
                    grouped_words = made[g][:].bitcast(F32).rearrange("p (n u) -> p n u", u=2)
                    nc.scalar.copy(
                        out=grouped_words[:, part * 2 * P : (part + 1) * 2 * P, :],
                        in_=bank[:].rearrange("p u n -> p n u"),
                    )
                    between(2 * first_half + second_half)
            return made

        def quantise(step, made):
            s, half = STEPS[step]
            for g, grouped in enumerate(made):
                nc.vector.quantize_mx(
                    out=codes[s][:, 2 * half + g, :].bitcast(FP8X4),
                    scales=scales[s][:, 2 * half + g, :],
                    in_=grouped[:],
                )

        def open_sums(half):
            sums = []
            for m in (2 * half, 2 * half + 1):
                acc = psum_acc.tile([P, ROWS], F32)
                sums.append((m, acc))
            return sums

        def matmul_passes(g, half, sums, passes):
            for c in passes:
                for m, acc in sums:
                    row = 2 * half + c // 2
                    first = (2 * (c % 2) + m % 2) * P
                    nc.tensor.matmul_mx(
                        out=acc[:],
                        lhsT=codes[0][:, row, first : first + P].bitcast(FP8X4),
                        lhsT_scale=scales[0][:, row, first : first + P],
                        rhs=codes[g + 1][:, c, :].bitcast(FP8X4),
                        rhs_scale=scales[g + 1][:, c, :],
                        start=(c == 0),
                        stop=(c == PASSES - 1),
                    )

        def store(dst, sums, result):
            first = sums[0][0] * P
            nc.sync.dma_start(
                out=dst[first : first + 2 * P, :].rearrange("(b p) f -> p b f", p=P),
                in_=result[:].rearrange("p (b h) d -> p b (h d)", b=2),
            )

        def square_sums(sums):
            squares = scratch.tile([P, 2 * HEADS, HEAD], BF16)
            sumsq = small.tile([P, 2 * HEADS], F32)
            for b, (m, acc) in enumerate(sums):
                for h in range(HEADS):
                    nc.scalar.activation(
                        out=squares[:, b * HEADS + h, :],
                        in_=acc[:, h * HEAD : (h + 1) * HEAD],
                        func=ACT.Square,
                        accum_out=sumsq[:, b * HEADS + h : b * HEADS + h + 1],
                    )
            return sumsq

        def norm_and_rope(g, sums, sumsq, between):
            dst, table = groups[g]
            inv_rms = small.tile([P, 2 * HEADS], F32)
            nc.scalar.activation(
                out=inv_rms[:],
                in_=sumsq[:],
                func=ACT.Abs_reciprocal_sqrt,
                scale=1.0 / HEAD,
                bias=eps[:, 0:1],
            )
            products = products_pool.tile([P, 2 * HEADS, 2, HEAD], F32)

            def multiply(b, h):
                m, acc = sums[b]
                nc.vector.scalar_tensor_tensor(
                    out=products[:, b * HEADS + h, :, :],
                    in0=acc[:, h * HEAD : (h + 1) * HEAD].unsqueeze(1).to_broadcast([P, 2, HEAD]),
                    scalar=inv_rms[:, b * HEADS + h : b * HEADS + h + 1],
                    in1=table[:, m % 2, :, :],
                    op0=ALU.mult,
                    op1=ALU.mult,
                )

            between()
            for b in range(2):
                for h in range(HEADS):
                    multiply(b, h)
            result = result_pool.tile([P, 2 * HEADS, HEAD], F32)
            nc.gpsimd.tensor_tensor(
                out=result[:, :, 0:HALF],
                in0=products[:, :, 0, 0:HALF],
                in1=products[:, :, 1, HALF:HEAD],
                op=ALU.subtract,
            )
            nc.gpsimd.tensor_tensor(
                out=result[:, :, HALF:HEAD],
                in0=products[:, :, 0, HALF:HEAD],
                in1=products[:, :, 1, 0:HALF],
                op=ALU.add,
            )
            store(dst, sums, result)

        def copy_values(g, sums):
            dst, table = groups[g]
            result = result_pool.tile([P, 2 * HEADS, HEAD], F32)
            for b, copy_out, queue in (
                (0, nc.scalar.copy, nc.scalar),
                (1, nc.vector.tensor_copy, nc.sync),
            ):
                m, acc = sums[b]
                flat = result[:, b * HEADS : (b + 1) * HEADS, :].rearrange("p h d -> p (h d)")
                copy_out(out=flat, in_=acc[:])
                queue.dma_start(out=dst[m * P : (m + 1) * P, :], in_=flat)

        n_matmuls = 2 * N_GROUPS
        plan = {LAG - 1: (0, (0, 1, 2, 3)), LAG: (1, (0, 1)), LAG + 1: (1, (2, 3))}
        for j in range(2, n_matmuls):
            plan[j + LAG] = (j, (0, 1, 2, 3))
        waiting = {}
        reorder(0)
        for i in range(n_matmuls + LAG + 1):
            def reorder_next():
                if i + 1 < len(STEPS):
                    reorder(i + 1)

            done, passes = plan.get(i - 1, (None, ()))
            sumsq = None
            if PASSES - 1 in passes:
                if groups[done // 2][1] is None:
                    copy_values(done // 2, waiting[done])
                else:
                    sumsq = square_sums(waiting[done])
            j, passes = plan.get(i, (None, ()))
            if 0 in passes:
                waiting[j] = open_sums(j % 2)

            def after_bank(n):
                if n == 0:
                    if sumsq is not None:
                        norm_and_rope(done // 2, waiting[done], sumsq, reorder_next)
                    else:
                        reorder_next()
                if n == 3 and passes:
                    matmul_passes(j // 2, j % 2, waiting[j], passes)

            made = []
            if i < len(STEPS):
                made = transpose(i, after_bank)
                if i + LOADS_AHEAD < len(STEPS):
                    load(i + LOADS_AHEAD)
            else:
                for n in range(4):
                    after_bank(n)
            if i < len(STEPS):
                quantise(i, made)
